import numpy as np
import ml_dtypes


def mxq(x, axis, fmt="e4m3"):
    dtype, down = {"e4m3": (ml_dtypes.float8_e4m3fn, 7), "e5m2": (ml_dtypes.float8_e5m2, 14)}[fmt]
    v = np.moveaxis(np.asarray(x, np.float32).astype(ml_dtypes.bfloat16).astype(np.float64), axis, -1)
    blocks = v.reshape(v.shape[:-1] + (-1, 32))
    amax = np.abs(blocks).max(-1, keepdims=True)
    byte = np.maximum(np.where(amax > 0, np.frexp(amax)[1] - 1 + 127, 0) - down, 1)
    scale = np.exp2(byte - 127.0)
    codes = (blocks / scale).astype(np.float32).astype(dtype).astype(np.float64)
    return np.moveaxis((codes * scale).reshape(v.shape), -1, axis)


WIDE = False


def mx_kscale(k):
    if not WIDE:
        return np.ones(k)
    levels = np.array([10, -10, 5, -5, 0])
    a = np.random.permutation(np.resize(levels, k // 512 * 4)).reshape(k // 512, 4)
    idx = np.arange(k)
    return np.exp2(a[idx // 512, idx % 128 // 32])


BF16 = ml_dtypes.bfloat16


def bf(x):
    return np.asarray(x, np.float32).astype(BF16)


def f64(x):
    return np.asarray(x).astype(np.float64)


I, B, D, H, F = 1024, 4, 512, 4, 128
EPS = 1e-5


def setup_inputs():
    s = mx_kscale(D)
    return {"x": bf(np.random.standard_normal((I, B, D))),
            "gamma": bf((1.0 + 0.1 * np.random.standard_normal(D)) * s),
            "beta": bf(0.1 * np.random.standard_normal(D) * s),
            "Wq": bf(np.random.standard_normal((D, H * F)) * 1.5 / np.sqrt(D) / s[:, None]),
            "Wv": bf(np.random.standard_normal((D, H * F)) * 1.5 / np.sqrt(D) / s[:, None]),
            "u_bias": bf(np.random.standard_normal((H, F)) * 0.5),
            "v_bias": bf(np.random.standard_normal((H, F)) * 0.5)}


def reference(x, gamma, beta, Wq, Wv, u_bias, v_bias):
    x = f64(x)
    mu = x.mean(-1, keepdims=True)
    var = ((x - mu) ** 2).mean(-1, keepdims=True)
    h = (x - mu) / np.sqrt(var + EPS) * f64(gamma) + f64(beta)
    hq = mxq(h, 2, "e4m3")
    q = (hq @ mxq(f64(Wq), 0, "e4m3")).reshape(I, B, H, F)
    v = (hq @ mxq(f64(Wv), 0, "e4m3")).reshape(I, B, H, F)
    return q + f64(u_bias), q + f64(v_bias), q, v

@@ -1,0 +1,251 @@
+import concourse.mybir as mybir
+from concourse.masks import make_identity
+
+F32 = mybir.dt.float32
+BF16 = mybir.dt.bfloat16
+U32 = mybir.dt.uint32
+U8 = mybir.dt.uint8
+FP8X4 = mybir.dt.float8_e4m3fn_x4
+ACT = mybir.ActivationFunctionType
+ALU = mybir.AluOpType
+
+P = 128
+D = 512
+PACK = 4
+ROWS = 1024 * 4
+ROW_TILES = ROWS // P
+GROUP = 2
+GROUPS = ROW_TILES // GROUP
+BANK = 512
+CHUNKS_PER_BANK = BANK // (GROUP * P)
+LOAD_TILES = 4
+RUN = 4
+EPS = 1e-5
+
+FLOPS = 2 * ROWS * D * (2 * D)
+
+
+def tile_multiheadattentiowithrpe_pa_t_kernel(
+    tc, x, gamma, beta, Wq, Wv, u_bias, v_bias, out_0, out_1, out_2, out_3
+):
+    nc = tc.nc
+    x_rows = x.rearrange("(p a) b d -> p (a b) d", p=P)
+    out_rows = [
+        o.rearrange("(p a) b h f -> p (a b) (h f)", p=P) for o in (out_0, out_1, out_2, out_3)
+    ]
+
+    with (
+        tc.tile_pool(name="keep", bufs=1) as keep,
+        tc.tile_pool(name="small", bufs=4) as small,
+        tc.tile_pool(name="work", bufs=2) as work,
+        tc.tile_pool(name="stage", bufs=5) as stage,
+        tc.psum_pool(name="psum", bufs=2) as psum,
+        tc.manual_schedule(),
+    ):
+        x_home = {}
+
+        def load_rows(first, count):
+            chunk = keep.tile([P, count, D], BF16, name="x_sb%d" % first)
+            nc.sync.dma_start(out=chunk[:], in_=x_rows[:, first : first + count, :])
+            for i in range(count):
+                x_home[first + i] = (chunk, i)
+
+        def load_weight(weight, name):
+            raw = keep.tile([P, PACK, D], BF16, name=name)
+            nc.sync.dma_start(out=raw[:], in_=weight.rearrange("(t p) n -> p t n", p=P))
+            return raw
+
+        load_rows(0, GROUP)
+        wq_raw = load_weight(Wq, "wq_raw")
+        load_rows(GROUP, GROUP)
+        wv_raw = load_weight(Wv, "wv_raw")
+        for first in range(2 * GROUP, ROW_TILES, LOAD_TILES):
+            load_rows(first, LOAD_TILES)
+        w_raw = [wq_raw, wv_raw]
+
+        vec_rows = keep.tile([P, P], BF16, name="vec_rows")
+        nc.vector.memset(vec_rows[:], 0.0)
+        bias_row = keep.tile([P, 2, D], BF16, name="bias_row")
+        nc.vector.memset(bias_row[:], 0.0)
+        ones = keep.tile([P, P], BF16, name="ones")
+        nc.vector.memset(ones[:], 1.0)
+        minus_half = keep.tile([P, GROUP, 1], F32, name="minus_half")
+        nc.vector.memset(minus_half[:], -0.5)
+        nc.scalar.dma_start(out=vec_rows[0:PACK, :], in_=gamma.rearrange("(t p) -> t p", p=P))
+        nc.scalar.dma_start(out=vec_rows[PACK : 2 * PACK, :], in_=beta.rearrange("(t p) -> t p", p=P))
+        nc.scalar.dma_start(out=bias_row[0:1, 0, :], in_=u_bias.rearrange("h f -> (h f)").unsqueeze(0))
+        nc.scalar.dma_start(out=bias_row[0:1, 1, :], in_=v_bias.rearrange("h f -> (h f)").unsqueeze(0))
+        ident = keep.tile([P, P], F32, name="ident")
+        make_identity(nc, ident[:])
+        gain_offset = keep.tile([P, 2 * PACK], F32, name="gain_offset")
+        biases = keep.tile([P, 2, D], F32, name="biases")
+        w_grouped = [
+            keep.tile([P, D, PACK], BF16, name="w_grouped%d" % w, align_bytes=64) for w in range(2)
+        ]
+        w_codes = keep.tile([P, 2, D], U32, name="w_codes", align_bytes=64)
+        w_scales = keep.tile([P, 2, D], U8, name="w_scales", align_bytes=64)
+
+        def turn_gamma_beta():
+            vec_rows_f32 = keep.tile([P, P], F32, name="vec_rows_f32")
+            nc.scalar.copy(out=vec_rows_f32[:], in_=vec_rows[:])
+            vec_cols = psum.tile([P, CHUNKS_PER_BANK, GROUP, P], F32, tag="turned", name="vec_cols")
+            nc.tensor.transpose(vec_cols[:, 0, 0, :], vec_rows_f32[:], ident[:])
+            nc.scalar.copy(out=gain_offset[:], in_=vec_cols[:, 0, 0, 0 : 2 * PACK])
+
+        def regroup_weights():
+            for w in range(2):
+                nc.scalar.copy(
+                    out=w_grouped[w][:].rearrange("p (c i) t -> p c t i", i=RUN),
+                    in_=w_raw[w][:].rearrange("p t (c i) -> p c t i", i=RUN),
+                )
+
+        def quantise_weights():
+            for w in range(2):
+                nc.vector.quantize_mx(
+                    out=w_codes[:, w, :].bitcast(FP8X4),
+                    scales=w_scales[:, w, :],
+                    in_=w_grouped[w][:].rearrange("p c t -> p (c t)"),
+                )
+
+        def spread_biases():
+            for b, tag in enumerate(("q_plain", "v_plain")):
+                bias_ps = psum.tile([P, D], F32, tag=tag, name="bias_ps")
+                nc.tensor.matmul(out=bias_ps[:], lhsT=ones[:], rhs=bias_row[:, b, :], start=True, stop=True)
+                nc.scalar.copy(out=biases[:, b, :], in_=bias_ps[:])
+
+        def rows_of(g):
+            homes = [x_home[g * GROUP + r] for r in range(GROUP)]
+            return [chunk[:, i, :] for chunk, i in homes]
+
+        live = {}
+
+        def row_statistics(g):
+            stats = small.tile([P, GROUP, 6], F32, tag="stats", name="stats")
+            for r, rows in enumerate(rows_of(g)):
+                nc.vector.bn_stats(out=stats[:, r, :], in_=rows)
+            live["stats", g] = stats
+
+        def mean_and_rstd(g):
+            mean_var = small.tile([P, GROUP, 2], F32, tag="mean_var", name="mean_var")
+            for r in range(GROUP):
+                nc.vector.bn_aggr(out=mean_var[:, r, :], in_=live["stats", g][:, r, :])
+            var_eps = small.tile([P, GROUP, 1], F32, tag="var_eps", name="var_eps")
+            nc.gpsimd.tensor_scalar(
+                out=var_eps[:], in0=mean_var[:, :, 1:2], scalar1=EPS, scalar2=None, op0=ALU.add
+            )
+            rstd = small.tile([P, GROUP, 1], F32, tag="rstd", name="rstd")
+            nc.gpsimd.tensor_tensor(out=rstd[:], in0=var_eps[:], in1=minus_half[:], op=ALU.pow)
+            live["mean_var", g] = mean_var
+            live["rstd", g] = rstd
+
+        def normalise(g):
+            normal = work.tile([P, GROUP, D], F32, tag="normal", name="normal")
+            for r, rows in enumerate(rows_of(g)):
+                nc.gpsimd.tensor_scalar(
+                    out=normal[:, r, :], in0=rows,
+                    scalar1=live["mean_var", g][:, r, 0:1], scalar2=live["rstd", g][:, r, :],
+                    op0=ALU.subtract, op1=ALU.mult,
+                )
+            live["normal", g] = normal
+
+        def turn(g):
+            banks = [
+                psum.tile([P, CHUNKS_PER_BANK, GROUP, P], F32, tag="turned", name="turned%d" % b)
+                for b in range(PACK // CHUNKS_PER_BANK)
+            ]
+            for r in range(GROUP):
+                for t in range(PACK):
+                    nc.tensor.transpose(
+                        banks[t // CHUNKS_PER_BANK][:, t % CHUNKS_PER_BANK, r, :],
+                        live["normal", g][:, r, t * P : (t + 1) * P],
+                        ident[:],
+                    )
+            live["turned", g] = banks
+
+        def scale_shift(g):
+            planes = work.tile([P, PACK, GROUP * P], BF16, tag="planes", name="planes")
+            for t in range(PACK):
+                bank = live["turned", g][t // CHUNKS_PER_BANK]
+                nc.scalar.activation(
+                    out=planes[:, t, :],
+                    in_=bank[:, t % CHUNKS_PER_BANK, :, :].rearrange("p r c -> p (r c)"),
+                    func=ACT.Identity,
+                    scale=gain_offset[:, t : t + 1],
+                    bias=gain_offset[:, PACK + t : PACK + t + 1],
+                )
+            live["planes", g] = planes
+
+        def quantise(g):
+            grouped = work.tile([P, GROUP * P, PACK], BF16, tag="grouped", name="grouped", align_bytes=64)
+            nc.vector.tensor_copy(
+                out=grouped[:].rearrange("p (c i) t -> p c t i", i=RUN),
+                in_=live["planes", g][:].rearrange("p t (c i) -> p c t i", i=RUN),
+            )
+            codes = work.tile([P, GROUP * P], U32, tag="codes", name="codes", align_bytes=64)
+            scales = work.tile([P, GROUP * P], U8, tag="scales", name="scales", align_bytes=64)
+            nc.vector.quantize_mx(
+                out=codes[:].bitcast(FP8X4),
+                scales=scales[:],
+                in_=grouped[:].rearrange("p c t -> p (c t)"),
+            )
+            live["codes", g] = codes
+            live["scales", g] = scales
+
+        def project(g):
+            for r in range(GROUP):
+                cols = slice(r * P, (r + 1) * P)
+                for tag, w in (("q_biased", 0), ("q_plain", 0), ("v_plain", 1)):
+                    acc = psum.tile([P, D], F32, tag=tag, name=tag)
+                    nc.tensor.matmul_mx(
+                        out=acc[:],
+                        lhsT=live["codes", g][:, cols].bitcast(FP8X4),
+                        lhsT_scale=live["scales", g][:, cols],
+                        rhs=w_codes[:, w, :].bitcast(FP8X4),
+                        rhs_scale=w_scales[:, w, :],
+                        start=True,
+                        stop=True,
+                    )
+                    live[tag, g, r] = acc
+
+        def finish(g):
+            biased = stage.tile([P, 2, GROUP, D], F32, tag="biased", name="biased")
+            plain = stage.tile([P, 2, GROUP, D], F32, tag="plain", name="plain")
+            for r in range(GROUP):
+                nc.vector.tensor_tensor(
+                    out=biased[:, :, r, :],
+                    in0=live["q_biased", g, r][:].unsqueeze(1).to_broadcast([P, 2, D]),
+                    in1=biases[:],
+                    op=ALU.add,
+                )
+                nc.scalar.copy(out=plain[:, 0, r, :], in_=live["q_plain", g, r][:])
+                nc.scalar.copy(out=plain[:, 1, r, :], in_=live["v_plain", g, r][:])
+            tiles = slice(g * GROUP, (g + 1) * GROUP)
+            nc.sync.dma_start(out=out_rows[2][:, tiles, :], in_=plain[:, 0, :, :])
+            nc.sync.dma_start(out=out_rows[3][:, tiles, :], in_=plain[:, 1, :, :])
+            nc.sync.dma_start(out=out_rows[0][:, tiles, :], in_=biased[:, 0, :, :])
+            nc.sync.dma_start(out=out_rows[1][:, tiles, :], in_=biased[:, 1, :, :])
+
+        turn_gamma_beta()
+        regroup_weights()
+        for arriving in range(GROUPS + 3):
+            turning = arriving - 1
+            packing = arriving - 2
+            leaving = arriving - 3
+            if 0 <= leaving:
+                project(leaving)
+            if 0 <= turning < GROUPS:
+                mean_and_rstd(turning)
+                normalise(turning)
+            if arriving < GROUPS:
+                row_statistics(arriving)
+            if 0 <= leaving:
+                finish(leaving)
+            if 0 <= turning < GROUPS:
+                turn(turning)
+                scale_shift(turning)
+            if turning == 0:
+                spread_biases()
+            if packing == 0:
+                quantise_weights()
+            if 0 <= packing < GROUPS:
+                quantise(packing)

@@ -135,16 +135,22 @@ def tile_multiheadattentiowithrpe_pa_t_kernel(
             )
             rstd = small.tile([P, GROUP, 1], F32, tag="rstd", name="rstd")
             nc.gpsimd.tensor_tensor(out=rstd[:], in0=var_eps[:], in1=minus_half[:], op=ALU.pow)
-            live["mean_var", g] = mean_var
+            mean_rstd = small.tile([P, GROUP, 1], F32, tag="mean_rstd", name="mean_rstd")
+            nc.gpsimd.tensor_tensor(out=mean_rstd[:], in0=mean_var[:, :, 0:1], in1=rstd[:], op=ALU.mult)
+            shift = small.tile([P, GROUP, 1], F32, tag="shift", name="shift")
+            nc.gpsimd.tensor_scalar(
+                out=shift[:], in0=mean_rstd[:], scalar1=-1.0, scalar2=0.0, op0=ALU.mult, op1=ALU.add
+            )
             live["rstd", g] = rstd
+            live["shift", g] = shift
 
         def normalise(g):
             normal = work.tile([P, GROUP, D], F32, tag="normal", name="normal")
             for r, rows in enumerate(rows_of(g)):
                 nc.gpsimd.tensor_scalar(
                     out=normal[:, r, :], in0=rows,
-                    scalar1=live["mean_var", g][:, r, 0:1], scalar2=live["rstd", g][:, r, :],
-                    op0=ALU.subtract, op1=ALU.mult,
+                    scalar1=live["rstd", g][:, r, :], scalar2=live["shift", g][:, r, :],
+                    op0=ALU.mult, op1=ALU.add,
                 )
             live["normal", g] = normal
 

@@ -69,12 +69,14 @@ def tile_multiheadattentiowithrpe_pa_t_kernel(
         nc.vector.memset(bias_row[:], 0.0)
         ones = keep.tile([P, P], BF16, name="ones")
         nc.vector.memset(ones[:], 1.0)
-        minus_half = keep.tile([P, GROUP, 1], F32, name="minus_half")
-        nc.vector.memset(minus_half[:], -0.5)
+        eps = keep.tile([P, 1], F32, name="eps")
+        nc.vector.memset(eps[:], EPS)
         nc.scalar.dma_start(out=vec_rows[0:PACK, :], in_=gamma.rearrange("(t p) -> t p", p=P))
         nc.scalar.dma_start(out=vec_rows[PACK : 2 * PACK, :], in_=beta.rearrange("(t p) -> t p", p=P))
         nc.scalar.dma_start(out=bias_row[0:1, 0, :], in_=u_bias.rearrange("h f -> (h f)").unsqueeze(0))
         nc.scalar.dma_start(out=bias_row[0:1, 1, :], in_=v_bias.rearrange("h f -> (h f)").unsqueeze(0))
+        warm = keep.tile([P, 1], F32, name="warm")
+        nc.scalar.activation(out=warm[:], in_=eps[:], func=ACT.Abs_reciprocal_sqrt)
         ident = keep.tile([P, P], F32, name="ident")
         make_identity(nc, ident[:])
         gain_offset = keep.tile([P, 2 * PACK], F32, name="gain_offset")
@@ -129,12 +131,10 @@ def tile_multiheadattentiowithrpe_pa_t_kernel(
             mean_var = small.tile([P, GROUP, 2], F32, tag="mean_var", name="mean_var")
             for r in range(GROUP):
                 nc.vector.bn_aggr(out=mean_var[:, r, :], in_=live["stats", g][:, r, :])
-            var_eps = small.tile([P, GROUP, 1], F32, tag="var_eps", name="var_eps")
-            nc.gpsimd.tensor_scalar(
-                out=var_eps[:], in0=mean_var[:, :, 1:2], scalar1=EPS, scalar2=None, op0=ALU.add
-            )
             rstd = small.tile([P, GROUP, 1], F32, tag="rstd", name="rstd")
-            nc.gpsimd.tensor_tensor(out=rstd[:], in0=var_eps[:], in1=minus_half[:], op=ALU.pow)
+            nc.scalar.activation(
+                out=rstd[:], in_=mean_var[:, :, 1:2], func=ACT.Abs_reciprocal_sqrt, bias=eps[:]
+            )
             mean_rstd = small.tile([P, GROUP, 1], F32, tag="mean_rstd", name="mean_rstd")
             nc.gpsimd.tensor_tensor(out=mean_rstd[:], in0=mean_var[:, :, 0:1], in1=rstd[:], op=ALU.mult)
             shift = small.tile([P, GROUP, 1], F32, tag="shift", name="shift")

@@ -56,8 +56,8 @@ def tile_multiheadattentiowithrpe_pa_t_kernel(
             return raw
 
         load_rows(0, GROUP)
-        wq_raw = load_weight(Wq, "wq_raw")
         load_rows(GROUP, GROUP)
+        wq_raw = load_weight(Wq, "wq_raw")
         wv_raw = load_weight(Wv, "wv_raw")
         for first in range(2 * GROUP, ROW_TILES, LOAD_TILES):
             load_rows(first, LOAD_TILES)
@@ -69,14 +69,12 @@ def tile_multiheadattentiowithrpe_pa_t_kernel(
         nc.vector.memset(bias_row[:], 0.0)
         ones = keep.tile([P, P], BF16, name="ones")
         nc.vector.memset(ones[:], 1.0)
-        eps = keep.tile([P, 1], F32, name="eps")
-        nc.vector.memset(eps[:], EPS)
+        minus_half = keep.tile([P, GROUP, 1], F32, name="minus_half")
+        nc.vector.memset(minus_half[:], -0.5)
         nc.scalar.dma_start(out=vec_rows[0:PACK, :], in_=gamma.rearrange("(t p) -> t p", p=P))
         nc.scalar.dma_start(out=vec_rows[PACK : 2 * PACK, :], in_=beta.rearrange("(t p) -> t p", p=P))
         nc.scalar.dma_start(out=bias_row[0:1, 0, :], in_=u_bias.rearrange("h f -> (h f)").unsqueeze(0))
         nc.scalar.dma_start(out=bias_row[0:1, 1, :], in_=v_bias.rearrange("h f -> (h f)").unsqueeze(0))
-        warm = keep.tile([P, 1], F32, name="warm")
-        nc.scalar.activation(out=warm[:], in_=eps[:], func=ACT.Abs_reciprocal_sqrt)
         ident = keep.tile([P, P], F32, name="ident")
         make_identity(nc, ident[:])
         gain_offset = keep.tile([P, 2 * PACK], F32, name="gain_offset")
@@ -94,14 +92,12 @@ def tile_multiheadattentiowithrpe_pa_t_kernel(
             nc.tensor.transpose(vec_cols[:, 0, 0, :], vec_rows_f32[:], ident[:])
             nc.scalar.copy(out=gain_offset[:], in_=vec_cols[:, 0, 0, 0 : 2 * PACK])
 
-        def regroup_weights():
+        def quantise_weights():
             for w in range(2):
-                nc.scalar.copy(
+                nc.vector.tensor_copy(
                     out=w_grouped[w][:].rearrange("p (c i) t -> p c t i", i=RUN),
                     in_=w_raw[w][:].rearrange("p t (c i) -> p c t i", i=RUN),
                 )
-
-        def quantise_weights():
             for w in range(2):
                 nc.vector.quantize_mx(
                     out=w_codes[:, w, :].bitcast(FP8X4),
@@ -131,10 +127,12 @@ def tile_multiheadattentiowithrpe_pa_t_kernel(
             mean_var = small.tile([P, GROUP, 2], F32, tag="mean_var", name="mean_var")
             for r in range(GROUP):
                 nc.vector.bn_aggr(out=mean_var[:, r, :], in_=live["stats", g][:, r, :])
-            rstd = small.tile([P, GROUP, 1], F32, tag="rstd", name="rstd")
-            nc.scalar.activation(
-                out=rstd[:], in_=mean_var[:, :, 1:2], func=ACT.Abs_reciprocal_sqrt, bias=eps[:]
+            var_eps = small.tile([P, GROUP, 1], F32, tag="var_eps", name="var_eps")
+            nc.gpsimd.tensor_scalar(
+                out=var_eps[:], in0=mean_var[:, :, 1:2], scalar1=EPS, scalar2=None, op0=ALU.add
             )
+            rstd = small.tile([P, GROUP, 1], F32, tag="rstd", name="rstd")
+            nc.gpsimd.tensor_tensor(out=rstd[:], in0=var_eps[:], in1=minus_half[:], op=ALU.pow)
             mean_rstd = small.tile([P, GROUP, 1], F32, tag="mean_rstd", name="mean_rstd")
             nc.gpsimd.tensor_tensor(out=mean_rstd[:], in0=mean_var[:, :, 0:1], in1=rstd[:], op=ALU.mult)
             shift = small.tile([P, GROUP, 1], F32, tag="shift", name="shift")
@@ -147,10 +145,9 @@ def tile_multiheadattentiowithrpe_pa_t_kernel(
         def normalise(g):
             normal = work.tile([P, GROUP, D], F32, tag="normal", name="normal")
             for r, rows in enumerate(rows_of(g)):
-                nc.gpsimd.tensor_scalar(
-                    out=normal[:, r, :], in0=rows,
-                    scalar1=live["rstd", g][:, r, :], scalar2=live["shift", g][:, r, :],
-                    op0=ALU.mult, op1=ALU.add,
+                nc.scalar.activation(
+                    out=normal[:, r, :], in_=rows, func=ACT.Identity,
+                    scale=live["rstd", g][:, r, :], bias=live["shift", g][:, r, :],
                 )
             live["normal", g] = normal
 
@@ -213,45 +210,49 @@ def tile_multiheadattentiowithrpe_pa_t_kernel(
                     )
                     live[tag, g, r] = acc
 
-        def finish(g):
-            biased = stage.tile([P, 2, GROUP, D], F32, tag="biased", name="biased")
-            plain = stage.tile([P, 2, GROUP, D], F32, tag="plain", name="plain")
-            for r in range(GROUP):
-                nc.vector.tensor_tensor(
-                    out=biased[:, :, r, :],
-                    in0=live["q_biased", g, r][:].unsqueeze(1).to_broadcast([P, 2, D]),
-                    in1=biases[:],
-                    op=ALU.add,
-                )
-                nc.scalar.copy(out=plain[:, 0, r, :], in_=live["q_plain", g, r][:])
-                nc.scalar.copy(out=plain[:, 1, r, :], in_=live["v_plain", g, r][:])
+        def finish(g, r):
+            if r == 0:
+                live["biased", g] = stage.tile([P, 2, GROUP, D], F32, tag="biased", name="biased")
+                live["plain", g] = stage.tile([P, 2, GROUP, D], F32, tag="plain", name="plain")
+            nc.vector.tensor_tensor(
+                out=live["biased", g][:, :, r, :],
+                in0=live["q_biased", g, r][:].unsqueeze(1).to_broadcast([P, 2, D]),
+                in1=biases[:],
+                op=ALU.add,
+            )
+            nc.scalar.copy(out=live["plain", g][:, 0, r, :], in_=live["q_plain", g, r][:])
+            nc.scalar.copy(out=live["plain", g][:, 1, r, :], in_=live["v_plain", g, r][:])
+
+        def store(g):
             tiles = slice(g * GROUP, (g + 1) * GROUP)
-            nc.sync.dma_start(out=out_rows[2][:, tiles, :], in_=plain[:, 0, :, :])
-            nc.sync.dma_start(out=out_rows[3][:, tiles, :], in_=plain[:, 1, :, :])
-            nc.sync.dma_start(out=out_rows[0][:, tiles, :], in_=biased[:, 0, :, :])
-            nc.sync.dma_start(out=out_rows[1][:, tiles, :], in_=biased[:, 1, :, :])
+            nc.sync.dma_start(out=out_rows[0][:, tiles, :], in_=live["biased", g][:, 0, :, :])
+            nc.sync.dma_start(out=out_rows[1][:, tiles, :], in_=live["biased", g][:, 1, :, :])
+            nc.sync.dma_start(out=out_rows[2][:, tiles, :], in_=live["plain", g][:, 0, :, :])
+            nc.sync.dma_start(out=out_rows[3][:, tiles, :], in_=live["plain", g][:, 1, :, :])
 
         turn_gamma_beta()
-        regroup_weights()
-        for arriving in range(GROUPS + 3):
-            turning = arriving - 1
-            packing = arriving - 2
-            leaving = arriving - 3
+        spread_biases()
+        for arriving in range(GROUPS + 4):
+            normalising = arriving - 1
+            turning = arriving - 2
+            packing = arriving - 3
+            leaving = arriving - 4
             if 0 <= leaving:
                 project(leaving)
-            if 0 <= turning < GROUPS:
-                mean_and_rstd(turning)
-                normalise(turning)
-            if arriving < GROUPS:
-                row_statistics(arriving)
-            if 0 <= leaving:
-                finish(leaving)
+            if 0 <= packing < GROUPS:
+                scale_shift(packing)
             if 0 <= turning < GROUPS:
                 turn(turning)
-                scale_shift(turning)
-            if turning == 0:
-                spread_biases()
-            if packing == 0:
-                quantise_weights()
+            if 0 <= leaving:
+                finish(leaving, 0)
+                finish(leaving, 1)
+                store(leaving)
+            if 0 <= normalising < GROUPS:
+                normalise(normalising)
             if 0 <= packing < GROUPS:
                 quantise(packing)
+            if arriving < GROUPS:
+                row_statistics(arriving)
+                mean_and_rstd(arriving)
+            if arriving == 1:
+                quantise_weights()

@@ -18,7 +18,7 @@ GROUP = 2
 GROUPS = ROW_TILES // GROUP
 BANK = 512
 CHUNKS_PER_BANK = BANK // (GROUP * P)
-LOAD_TILES = 4
+LOAD_GROUPS = 2
 RUN = 4
 EPS = 1e-5
 
@@ -29,9 +29,10 @@ def tile_multiheadattentiowithrpe_pa_t_kernel(
     tc, x, gamma, beta, Wq, Wv, u_bias, v_bias, out_0, out_1, out_2, out_3
 ):
     nc = tc.nc
-    x_rows = x.rearrange("(p a) b d -> p (a b) d", p=P)
-    out_rows = [
-        o.rearrange("(p a) b h f -> p (a b) (h f)", p=P) for o in (out_0, out_1, out_2, out_3)
+    x_groups = x.rearrange("i b d -> (i b) d").rearrange("(g p r) d -> p g r d", p=P, r=GROUP)
+    out_groups = [
+        o.rearrange("i b h f -> (i b) (h f)").rearrange("(g p r) n -> p g r n", p=P, r=GROUP)
+        for o in (out_0, out_1, out_2, out_3)
     ]
 
     with (
@@ -44,9 +45,9 @@ def tile_multiheadattentiowithrpe_pa_t_kernel(
     ):
         x_home = {}
 
-        def load_rows(first, count):
-            chunk = keep.tile([P, count, D], BF16, name="x_sb%d" % first)
-            nc.sync.dma_start(out=chunk[:], in_=x_rows[:, first : first + count, :])
+        def load_groups(first, count):
+            chunk = keep.tile([P, count, GROUP, D], BF16, name="x_sb%d" % first)
+            nc.sync.dma_start(out=chunk[:], in_=x_groups[:, first : first + count, :, :])
             for i in range(count):
                 x_home[first + i] = (chunk, i)
 
@@ -55,12 +56,12 @@ def tile_multiheadattentiowithrpe_pa_t_kernel(
             nc.sync.dma_start(out=raw[:], in_=weight.rearrange("(t p) n -> p t n", p=P))
             return raw
 
-        load_rows(0, GROUP)
-        load_rows(GROUP, GROUP)
+        load_groups(0, 1)
+        load_groups(1, 1)
         wq_raw = load_weight(Wq, "wq_raw")
         wv_raw = load_weight(Wv, "wv_raw")
-        for first in range(2 * GROUP, ROW_TILES, LOAD_TILES):
-            load_rows(first, LOAD_TILES)
+        for first in range(2, GROUPS, LOAD_GROUPS):
+            load_groups(first, LOAD_GROUPS)
         w_raw = [wq_raw, wv_raw]
 
         vec_rows = keep.tile([P, P], BF16, name="vec_rows")
@@ -112,8 +113,8 @@ def tile_multiheadattentiowithrpe_pa_t_kernel(
                 nc.scalar.copy(out=biases[:, b, :], in_=bias_ps[:])
 
         def rows_of(g):
-            homes = [x_home[g * GROUP + r] for r in range(GROUP)]
-            return [chunk[:, i, :] for chunk, i in homes]
+            chunk, i = x_home[g]
+            return [chunk[:, i, r, :] for r in range(GROUP)]
 
         live = {}
 
@@ -224,11 +225,10 @@ def tile_multiheadattentiowithrpe_pa_t_kernel(
             nc.scalar.copy(out=live["plain", g][:, 1, r, :], in_=live["v_plain", g, r][:])
 
         def store(g):
-            tiles = slice(g * GROUP, (g + 1) * GROUP)
-            nc.sync.dma_start(out=out_rows[0][:, tiles, :], in_=live["biased", g][:, 0, :, :])
-            nc.sync.dma_start(out=out_rows[1][:, tiles, :], in_=live["biased", g][:, 1, :, :])
-            nc.sync.dma_start(out=out_rows[2][:, tiles, :], in_=live["plain", g][:, 0, :, :])
-            nc.sync.dma_start(out=out_rows[3][:, tiles, :], in_=live["plain", g][:, 1, :, :])
+            nc.sync.dma_start(out=out_groups[0][:, g, :, :], in_=live["biased", g][:, 0, :, :])
+            nc.sync.dma_start(out=out_groups[1][:, g, :, :], in_=live["biased", g][:, 1, :, :])
+            nc.sync.dma_start(out=out_groups[2][:, g, :, :], in_=live["plain", g][:, 0, :, :])
+            nc.sync.dma_start(out=out_groups[3][:, g, :, :], in_=live["plain", g][:, 1, :, :])
 
         turn_gamma_beta()
         spread_biases()

import concourse.mybir as mybir
from concourse.masks import make_identity

F32 = mybir.dt.float32
BF16 = mybir.dt.bfloat16
U32 = mybir.dt.uint32
U8 = mybir.dt.uint8
FP8X4 = mybir.dt.float8_e4m3fn_x4
ACT = mybir.ActivationFunctionType
ALU = mybir.AluOpType

P = 128
D = 512
PACK = 4
ROWS = 1024 * 4
ROW_TILES = ROWS // P
GROUP = 2
GROUPS = ROW_TILES // GROUP
BANK = 512
CHUNKS_PER_BANK = BANK // (GROUP * P)
LOAD_GROUPS = 2
RUN = 4
EPS = 1e-5

FLOPS = 2 * ROWS * D * (2 * D)


def tile_multiheadattentiowithrpe_pa_t_kernel(
    tc, x, gamma, beta, Wq, Wv, u_bias, v_bias, out_0, out_1, out_2, out_3
):
    nc = tc.nc
    x_groups = x.rearrange("i b d -> (i b) d").rearrange("(g p r) d -> p g r d", p=P, r=GROUP)
    out_groups = [
        o.rearrange("i b h f -> (i b) (h f)").rearrange("(g p r) n -> p g r n", p=P, r=GROUP)
        for o in (out_0, out_1, out_2, out_3)
    ]

    with (
        tc.tile_pool(name="keep", bufs=1) as keep,
        tc.tile_pool(name="small", bufs=4) as small,
        tc.tile_pool(name="work", bufs=2) as work,
        tc.tile_pool(name="stage", bufs=5) as stage,
        tc.psum_pool(name="psum", bufs=2) as psum,
        tc.manual_schedule(),
    ):
        x_home = {}

        def load_groups(first, count):
            chunk = keep.tile([P, count, GROUP, D], BF16, name="x_sb%d" % first)
            nc.sync.dma_start(out=chunk[:], in_=x_groups[:, first : first + count, :, :])
            for i in range(count):
                x_home[first + i] = (chunk, i)

        def load_weight(weight, name):
            raw = keep.tile([P, PACK, D], BF16, name=name)
            nc.sync.dma_start(out=raw[:], in_=weight.rearrange("(t p) n -> p t n", p=P))
            return raw

        load_groups(0, 1)
        load_groups(1, 1)
        wq_raw = load_weight(Wq, "wq_raw")
        wv_raw = load_weight(Wv, "wv_raw")
        for first in range(2, GROUPS, LOAD_GROUPS):
            load_groups(first, LOAD_GROUPS)
        w_raw = [wq_raw, wv_raw]

        vec_rows = keep.tile([P, P], BF16, name="vec_rows")
        nc.vector.memset(vec_rows[:], 0.0)
        bias_row = keep.tile([P, 2, D], BF16, name="bias_row")
        nc.vector.memset(bias_row[:], 0.0)
        ones = keep.tile([P, P], BF16, name="ones")
        nc.vector.memset(ones[:], 1.0)
        minus_half = keep.tile([P, GROUP, 1], F32, name="minus_half")
        nc.vector.memset(minus_half[:], -0.5)
        nc.scalar.dma_start(out=vec_rows[0:PACK, :], in_=gamma.rearrange("(t p) -> t p", p=P))
        nc.scalar.dma_start(out=vec_rows[PACK : 2 * PACK, :], in_=beta.rearrange("(t p) -> t p", p=P))
        nc.scalar.dma_start(out=bias_row[0:1, 0, :], in_=u_bias.rearrange("h f -> (h f)").unsqueeze(0))
        nc.scalar.dma_start(out=bias_row[0:1, 1, :], in_=v_bias.rearrange("h f -> (h f)").unsqueeze(0))
        ident = keep.tile([P, P], F32, name="ident")
        make_identity(nc, ident[:])
        gain_offset = keep.tile([P, 2 * PACK], F32, name="gain_offset")
        biases = keep.tile([P, 2, D], F32, name="biases")
        w_grouped = [
            keep.tile([P, D, PACK], BF16, name="w_grouped%d" % w, align_bytes=64) for w in range(2)
        ]
        w_codes = keep.tile([P, 2, D], U32, name="w_codes", align_bytes=64)
        w_scales = keep.tile([P, 2, D], U8, name="w_scales", align_bytes=64)

        def turn_gamma_beta():
            vec_rows_f32 = keep.tile([P, P], F32, name="vec_rows_f32")
            nc.scalar.copy(out=vec_rows_f32[:], in_=vec_rows[:])
            vec_cols = psum.tile([P, CHUNKS_PER_BANK, GROUP, P], F32, tag="turned", name="vec_cols")
            nc.tensor.transpose(vec_cols[:, 0, 0, :], vec_rows_f32[:], ident[:])
            nc.scalar.copy(out=gain_offset[:], in_=vec_cols[:, 0, 0, 0 : 2 * PACK])

        def quantise_weights():
            for w in range(2):
                nc.vector.tensor_copy(
                    out=w_grouped[w][:].rearrange("p (c i) t -> p c t i", i=RUN),
                    in_=w_raw[w][:].rearrange("p t (c i) -> p c t i", i=RUN),
                )
            for w in range(2):
                nc.vector.quantize_mx(
                    out=w_codes[:, w, :].bitcast(FP8X4),
                    scales=w_scales[:, w, :],
                    in_=w_grouped[w][:].rearrange("p c t -> p (c t)"),
                )

        def spread_biases():
            for b, tag in enumerate(("q_plain", "v_plain")):
                bias_ps = psum.tile([P, D], F32, tag=tag, name="bias_ps")
                nc.tensor.matmul(out=bias_ps[:], lhsT=ones[:], rhs=bias_row[:, b, :], start=True, stop=True)
                nc.scalar.copy(out=biases[:, b, :], in_=bias_ps[:])

        def rows_of(g):
            chunk, i = x_home[g]
            return [chunk[:, i, r, :] for r in range(GROUP)]

        live = {}

        def row_statistics(g):
            stats = small.tile([P, GROUP, 6], F32, tag="stats", name="stats")
            for r, rows in enumerate(rows_of(g)):
                nc.vector.bn_stats(out=stats[:, r, :], in_=rows)
            live["stats", g] = stats

        def mean_and_rstd(g):
            mean_var = small.tile([P, GROUP, 2], F32, tag="mean_var", name="mean_var")
            for r in range(GROUP):
                nc.vector.bn_aggr(out=mean_var[:, r, :], in_=live["stats", g][:, r, :])
            var_eps = small.tile([P, GROUP, 1], F32, tag="var_eps", name="var_eps")
            nc.gpsimd.tensor_scalar(
                out=var_eps[:], in0=mean_var[:, :, 1:2], scalar1=EPS, scalar2=None, op0=ALU.add
            )
            rstd = small.tile([P, GROUP, 1], F32, tag="rstd", name="rstd")
            nc.gpsimd.tensor_tensor(out=rstd[:], in0=var_eps[:], in1=minus_half[:], op=ALU.pow)
            mean_rstd = small.tile([P, GROUP, 1], F32, tag="mean_rstd", name="mean_rstd")
            nc.gpsimd.tensor_tensor(out=mean_rstd[:], in0=mean_var[:, :, 0:1], in1=rstd[:], op=ALU.mult)
            shift = small.tile([P, GROUP, 1], F32, tag="shift", name="shift")
            nc.gpsimd.tensor_scalar(
                out=shift[:], in0=mean_rstd[:], scalar1=-1.0, scalar2=0.0, op0=ALU.mult, op1=ALU.add
            )
            live["rstd", g] = rstd
            live["shift", g] = shift

        def normalise(g):
            normal = work.tile([P, GROUP, D], F32, tag="normal", name="normal")
            for r, rows in enumerate(rows_of(g)):
                nc.scalar.activation(
                    out=normal[:, r, :], in_=rows, func=ACT.Identity,
                    scale=live["rstd", g][:, r, :], bias=live["shift", g][:, r, :],
                )
            live["normal", g] = normal

        def turn(g):
            banks = [
                psum.tile([P, CHUNKS_PER_BANK, GROUP, P], F32, tag="turned", name="turned%d" % b)
                for b in range(PACK // CHUNKS_PER_BANK)
            ]
            for r in range(GROUP):
                for t in range(PACK):
                    nc.tensor.transpose(
                        banks[t // CHUNKS_PER_BANK][:, t % CHUNKS_PER_BANK, r, :],
                        live["normal", g][:, r, t * P : (t + 1) * P],
                        ident[:],
                    )
            live["turned", g] = banks

        def scale_shift(g):
            planes = work.tile([P, PACK, GROUP * P], BF16, tag="planes", name="planes")
            for t in range(PACK):
                bank = live["turned", g][t // CHUNKS_PER_BANK]
                nc.scalar.activation(
                    out=planes[:, t, :],
                    in_=bank[:, t % CHUNKS_PER_BANK, :, :].rearrange("p r c -> p (r c)"),
                    func=ACT.Identity,
                    scale=gain_offset[:, t : t + 1],
                    bias=gain_offset[:, PACK + t : PACK + t + 1],
                )
            live["planes", g] = planes

        def quantise(g):
            grouped = work.tile([P, GROUP * P, PACK], BF16, tag="grouped", name="grouped", align_bytes=64)
            nc.vector.tensor_copy(
                out=grouped[:].rearrange("p (c i) t -> p c t i", i=RUN),
                in_=live["planes", g][:].rearrange("p t (c i) -> p c t i", i=RUN),
            )
            codes = work.tile([P, GROUP * P], U32, tag="codes", name="codes", align_bytes=64)
            scales = work.tile([P, GROUP * P], U8, tag="scales", name="scales", align_bytes=64)
            nc.vector.quantize_mx(
                out=codes[:].bitcast(FP8X4),
                scales=scales[:],
                in_=grouped[:].rearrange("p c t -> p (c t)"),
            )
            live["codes", g] = codes
            live["scales", g] = scales

        def project(g):
            for r in range(GROUP):
                cols = slice(r * P, (r + 1) * P)
                for tag, w in (("q_biased", 0), ("q_plain", 0), ("v_plain", 1)):
                    acc = psum.tile([P, D], F32, tag=tag, name=tag)
                    nc.tensor.matmul_mx(
                        out=acc[:],
                        lhsT=live["codes", g][:, cols].bitcast(FP8X4),
                        lhsT_scale=live["scales", g][:, cols],
                        rhs=w_codes[:, w, :].bitcast(FP8X4),
                        rhs_scale=w_scales[:, w, :],
                        start=True,
                        stop=True,
                    )
                    live[tag, g, r] = acc

        def finish(g, r):
            if r == 0:
                live["biased", g] = stage.tile([P, 2, GROUP, D], F32, tag="biased", name="biased")
                live["plain", g] = stage.tile([P, 2, GROUP, D], F32, tag="plain", name="plain")
            nc.vector.tensor_tensor(
                out=live["biased", g][:, :, r, :],
                in0=live["q_biased", g, r][:].unsqueeze(1).to_broadcast([P, 2, D]),
                in1=biases[:],
                op=ALU.add,
            )
            nc.scalar.copy(out=live["plain", g][:, 0, r, :], in_=live["q_plain", g, r][:])
            nc.scalar.copy(out=live["plain", g][:, 1, r, :], in_=live["v_plain", g, r][:])

        def store(g):
            nc.sync.dma_start(out=out_groups[0][:, g, :, :], in_=live["biased", g][:, 0, :, :])
            nc.sync.dma_start(out=out_groups[1][:, g, :, :], in_=live["biased", g][:, 1, :, :])
            nc.sync.dma_start(out=out_groups[2][:, g, :, :], in_=live["plain", g][:, 0, :, :])
            nc.sync.dma_start(out=out_groups[3][:, g, :, :], in_=live["plain", g][:, 1, :, :])

        turn_gamma_beta()
        spread_biases()
        for arriving in range(GROUPS + 4):
            normalising = arriving - 1
            turning = arriving - 2
            packing = arriving - 3
            leaving = arriving - 4
            if 0 <= leaving:
                project(leaving)
            if 0 <= packing < GROUPS:
                scale_shift(packing)
            if 0 <= turning < GROUPS:
                turn(turning)
            if 0 <= leaving:
                finish(leaving, 0)
                finish(leaving, 1)
                store(leaving)
            if 0 <= normalising < GROUPS:
                normalise(normalising)
            if 0 <= packing < GROUPS:
                quantise(packing)
            if arriving < GROUPS:
                row_statistics(arriving)
                mean_and_rstd(arriving)
            if arriving == 1:
                quantise_weights()
